import numpy as np
import ml_dtypes


def mxq(x, axis, fmt="e4m3"):
    dtype, down = {"e4m3": (ml_dtypes.float8_e4m3fn, 7), "e5m2": (ml_dtypes.float8_e5m2, 14)}[fmt]
    v = np.moveaxis(np.asarray(x, np.float32).astype(ml_dtypes.bfloat16).astype(np.float64), axis, -1)
    blocks = v.reshape(v.shape[:-1] + (-1, 32))
    amax = np.abs(blocks).max(-1, keepdims=True)
    byte = np.maximum(np.where(amax > 0, np.frexp(amax)[1] - 1 + 127, 0) - down, 1)
    scale = np.exp2(byte - 127.0)
    codes = (blocks / scale).astype(np.float32).astype(dtype).astype(np.float64)
    return np.moveaxis((codes * scale).reshape(v.shape), -1, axis)


WIDE = False


def mx_kscale(k):
    if not WIDE:
        return np.ones(k)
    levels = np.array([10, -10, 5, -5, 0])
    a = np.random.permutation(np.resize(levels, k // 512 * 4)).reshape(k // 512, 4)
    idx = np.arange(k)
    return np.exp2(a[idx // 512, idx % 128 // 32])


BF16 = ml_dtypes.bfloat16


def bf(x):
    return np.asarray(x, np.float32).astype(BF16)


def f64(x):
    return np.asarray(x).astype(np.float64)


B, H, S, D = 8, 2, 512, 256
D2 = D // 2
LAMBDA_INIT = 0.8
EPS = 1e-5


def softmax(v):
    e = np.exp(v - v.max(-1, keepdims=True))
    return e / e.sum(-1, keepdims=True)


def setup_inputs():
    s = mx_kscale(S)
    c = np.log(2.0) * np.sqrt(D2)
    q = np.random.standard_normal((B, H, S, D))
    k = np.random.standard_normal((B, H, S, D))
    q[..., 0] = c
    q[..., D2] = c
    k[..., 0] += np.log2(s)
    k[..., D2] += np.log2(s)
    v = np.random.standard_normal((B, H, S, D)) * 0.005 * np.sqrt(S) / s[:, None] * s.mean()
    return {"query": bf(q), "key": bf(k), "value": bf(v),
            "lambda_params": bf(0.3 + 0.5 * np.random.random(H))}


def reference(query, key, value, lambda_params):
    query, key, value, lambda_params = f64(query), f64(key), f64(value), f64(lambda_params)
    scale = 1.0 / np.sqrt(D2)
    q1, q2 = query[..., :D2], query[..., D2:]
    k1, k2 = key[..., :D2], key[..., D2:]
    a1 = softmax(q1 @ k1.transpose(0, 1, 3, 2) * scale)
    a2 = softmax(q2 @ k2.transpose(0, 1, 3, 2) * scale)
    lam = lambda_params[None, :, None, None]
    attn = a1 - lam * a2
    out = mxq(attn, 3, "e4m3") @ mxq(value, 2, "e4m3")
    mean = out.mean(-1, keepdims=True)
    var = ((out - mean) ** 2).mean(-1, keepdims=True)
    out = (out - mean) / np.sqrt(var + EPS)
    return out * (1.0 - LAMBDA_INIT)

@@ -1,0 +1,297 @@
+from contextlib import ExitStack
+import math
+
+import concourse.bass as bass
+import concourse.mybir as mybir
+import concourse.tile as tile
+from concourse.masks import make_identity
+
+F32 = mybir.dt.float32
+BF16 = mybir.dt.bfloat16
+U32 = mybir.dt.uint32
+U8 = mybir.dt.uint8
+FP8X4 = mybir.dt.float8_e4m3fn_x4
+ALU = mybir.AluOpType
+ACT = mybir.ActivationFunctionType
+AX = mybir.AxisListType
+
+P = 128
+HEADS = 16
+S = 512
+D = 256
+D2 = 128
+QB = 4
+UNITS = HEADS * QB
+SCALE = 1.0 / math.sqrt(D2)
+EPS = 1e-5
+GAIN = 1.0 - 0.8
+FLOPS = HEADS * (2 * 2 * S * S * D2 + 2 * S * S * D)
+
+MANUAL = False
+T_ON_G = True
+
+
+def tile_differentialattention_t_kernel(tc, query, key, value, lambda_params, out):
+    nc = tc.nc
+    qv = query.rearrange("b h s d -> (b h) s d")
+    kv = key.rearrange("b h s d -> (b h) s d")
+    vv = value.rearrange("b h s d -> (b h) s d")
+    ov = out.rearrange("b h s d -> (b h) s d")
+
+    with ExitStack() as ctx:
+        const = ctx.enter_context(tc.tile_pool(name="const", bufs=1))
+        ld = ctx.enter_context(tc.tile_pool(name="ld", bufs=4))
+        tsb = ctx.enter_context(tc.tile_pool(name="tsb", bufs=3))
+        vq = ctx.enter_context(tc.tile_pool(name="vq", bufs=3))
+        ep = ctx.enter_context(tc.tile_pool(name="ep", bufs=4))
+        ap = ctx.enter_context(tc.tile_pool(name="ap", bufs=4))
+        gp = ctx.enter_context(tc.tile_pool(name="gp", bufs=3))
+        sm = ctx.enter_context(tc.tile_pool(name="sm", bufs=6))
+        op = ctx.enter_context(tc.tile_pool(name="op", bufs=3))
+        ps_s = ctx.enter_context(tc.psum_pool(name="ps_s", bufs=4))
+        ps_t = ctx.enter_context(tc.psum_pool(name="ps_t", bufs=2))
+        ps_o = ctx.enter_context(tc.psum_pool(name="ps_o", bufs=2))
+
+        ident = const.tile([P, P], BF16, name="ident")
+        make_identity(nc, ident[:])
+        lam_bf = const.tile([P, 2], BF16, name="lam_bf")
+        nc.sync.dma_start(out=lam_bf[:], in_=lambda_params.partition_broadcast(P))
+        lam = const.tile([P, 2], F32, name="lam")
+        nc.vector.tensor_copy(out=lam[:], in_=lam_bf[:])
+        neghalf = const.tile([P, 2, 1], F32, name="neghalf")
+        nc.gpsimd.memset(neghalf[:], -0.5)
+
+        if MANUAL:
+            ctx.enter_context(tc.manual_schedule())
+
+        q_sb = {}
+        k_sb = {}
+        v_sb = {}
+        qT = {}
+        kT = {}
+        v_codes = {}
+        v_scales = {}
+        s_ps = {}
+        nbias = {}
+        sums = {}
+        rec = {}
+        e_sb = {}
+        attn = {}
+        aT = {}
+        grp = {}
+        a_codes = {}
+        a_scales = {}
+        o_ps = {}
+        mv = {}
+        ln_scale = {}
+        ln_bias = {}
+        o_sb = {}
+
+        def load(h):
+            tq = ld.tile([P, QB, D], BF16, name="tq", tag="q")
+            nc.sync.dma_start(out=tq[:], in_=qv[h].rearrange("(p t) d -> p t d", t=QB))
+            tk = ld.tile([P, QB, D], BF16, name="tk", tag="k")
+            nc.sync.dma_start(out=tk[:], in_=kv[h].rearrange("(t p) d -> p t d", p=P))
+            tv = ld.tile([P, QB, D], BF16, name="tv", tag="v")
+            nc.sync.dma_start(out=tv[:], in_=vv[h].rearrange("(t p) d -> p t d", p=P))
+            q_sb[h] = tq
+            k_sb[h] = tk
+            v_sb[h] = tv
+
+        def flip_pe(src):
+            tp = ps_t.tile([P, 2, S], BF16, name="tp", tag="tr")
+            for hf in range(2):
+                for t in range(QB):
+                    nc.tensor.transpose(
+                        tp[:, hf, t * P:(t + 1) * P], src[:, t, hf * D2:(hf + 1) * D2], ident[:]
+                    )
+            return tp
+
+        def flip_out(tp, tag):
+            dst = tsb.tile([P, 2, S], BF16, name="dst", tag=tag)
+            nc.scalar.copy(out=dst[:], in_=tp[:])
+            return dst
+
+        def value_quant(h):
+            vg = vq.tile([P, D, 4], BF16, name="vg", tag="vg", align_bytes=64)
+            nc.vector.tensor_copy(
+                out=vg[:].rearrange("p (c i) t -> p c t i", i=4),
+                in_=v_sb[h][:].rearrange("p t (c i) -> p c t i", i=4),
+            )
+            vc = vq.tile([P, D], U32, name="vc", tag="vc", align_bytes=64)
+            vs = vq.tile([P, D], U8, name="vs", tag="vs", align_bytes=64)
+            nc.vector.quantize_mx(
+                out=vc[:].bitcast(FP8X4), scales=vs[:], in_=vg[:].rearrange("p f t -> p (f t)")
+            )
+            v_codes[h] = vc
+            v_scales[h] = vs
+
+        def scores(u):
+            h, t = divmod(u, QB)
+            for hf in range(2):
+                sp = ps_s.tile([P, S], F32, name="sp", tag="s")
+                nc.tensor.matmul(
+                    sp[:], lhsT=qT[h][:, hf, t * P:(t + 1) * P], rhs=kT[h][:, hf, :],
+                    start=True, stop=True,
+                )
+                s_ps[(u, hf)] = sp
+
+        def row_max(u):
+            mx = sm.tile([P, 2], F32, name="mx", tag="mx")
+            for hf in range(2):
+                nc.vector.tensor_reduce(out=mx[:, hf:hf + 1], in_=s_ps[(u, hf)][:], axis=AX.X, op=ALU.max)
+            nb = sm.tile([P, 2], F32, name="nb", tag="nb")
+            nc.vector.tensor_scalar(out=nb[:], in0=mx[:], scalar1=-SCALE, scalar2=None, op0=ALU.mult)
+            nbias[u] = nb
+
+        def exps(u):
+            su = sm.tile([P, 2], F32, name="su", tag="su")
+            for hf in range(2):
+                e = ep.tile([P, S], F32, name="e", tag="e%d" % hf)
+                nc.scalar.activation(
+                    out=e[:], in_=s_ps[(u, hf)][:], func=ACT.Exp,
+                    bias=nbias[u][:, hf:hf + 1], scale=SCALE, accum_out=su[:, hf:hf + 1],
+                )
+                e_sb[(u, hf)] = e
+            sums[u] = su
+
+        def recip(u):
+            r = sm.tile([P, 2], F32, name="r", tag="r")
+            nc.vector.reciprocal(out=r[:], in_=sums[u][:])
+            rec[u] = r
+
+        def scale2(u):
+            h = u // QB
+            eng = nc.gpsimd if T_ON_G else nc.vector
+            e2 = e_sb[(u, 1)]
+            eng.tensor_scalar(
+                out=e2[:], in0=e2[:], scalar1=rec[u][:, 1:2], scalar2=lam[:, (h % 2):(h % 2) + 1],
+                op0=ALU.mult, op1=ALU.mult,
+            )
+
+        def combine(u):
+            at = ap.tile([P, S], BF16, name="at", tag="at")
+            nc.vector.scalar_tensor_tensor(
+                out=at[:], in0=e_sb[(u, 0)][:], scalar=rec[u][:, 0:1], in1=e_sb[(u, 1)][:],
+                op0=ALU.mult, op1=ALU.subtract,
+            )
+            attn[u] = at
+
+        def attn_flip(u):
+            tp = ps_t.tile([P, QB, P], BF16, name="tpa", tag="tr")
+            for t in range(QB):
+                nc.tensor.transpose(tp[:, t, :], attn[u][:, t * P:(t + 1) * P], ident[:])
+            aT[u] = tp
+
+        def attn_out(u):
+            pr, j = divmod(u, 2)
+            if j == 0:
+                g = gp.tile([P, 2, P, 4], BF16, name="g", tag="g", align_bytes=64)
+                grp[pr] = g
+            nc.scalar.copy(out=grp[pr][:, j, :, :], in_=aT[u][:].rearrange("p t q -> p q t"))
+
+        def attn_quant(pr):
+            ac = gp.tile([P, 2 * P], U32, name="ac", tag="ac", align_bytes=64)
+            asc = gp.tile([P, 2 * P], U8, name="asc", tag="asc", align_bytes=64)
+            nc.vector.quantize_mx(
+                out=ac[:].bitcast(FP8X4), scales=asc[:], in_=grp[pr][:].rearrange("p j q t -> p (j q t)")
+            )
+            a_codes[pr] = ac
+            a_scales[pr] = asc
+
+        def product(pr):
+            h = pr // 2
+            o = ps_o.tile([P, 2, D], F32, name="o", tag="o")
+            for j in range(2):
+                nc.tensor.matmul_mx(
+                    out=o[:, j, :],
+                    lhsT=a_codes[pr][:, j * P:(j + 1) * P].bitcast(FP8X4),
+                    lhsT_scale=a_scales[pr][:, j * P:(j + 1) * P],
+                    rhs=v_codes[h][:].bitcast(FP8X4),
+                    rhs_scale=v_scales[h][:],
+                    start=True, stop=True,
+                )
+            o_ps[pr] = o
+
+        def stats(pr):
+            st = sm.tile([P, 2, 6], F32, name="st", tag="st")
+            m = sm.tile([P, 2, 2], F32, name="m", tag="m")
+            for j in range(2):
+                nc.vector.bn_stats(out=st[:, j, :], in_=o_ps[pr][:, j, :])
+            for j in range(2):
+                nc.vector.bn_aggr(out=m[:, j, :], in_=st[:, j, :])
+            mv[pr] = m
+
+        def norm_consts(pr):
+            a = sm.tile([P, 2, 1], F32, name="a", tag="a")
+            nc.gpsimd.tensor_scalar(
+                out=a[:], in0=mv[pr][:, :, 1:2], scalar1=1.0 / (GAIN * GAIN), scalar2=EPS / (GAIN * GAIN),
+                op0=ALU.mult, op1=ALU.add,
+            )
+            nm = sm.tile([P, 2, 1], F32, name="nm", tag="nm")
+            nc.gpsimd.tensor_scalar(
+                out=nm[:], in0=mv[pr][:, :, 0:1], scalar1=-1.0, scalar2=0.0, op0=ALU.mult, op1=ALU.add
+            )
+            rs = sm.tile([P, 2, 1], F32, name="rs", tag="rs")
+            nc.gpsimd.tensor_tensor(out=rs[:], in0=a[:], in1=neghalf[:], op=ALU.pow)
+            lb = sm.tile([P, 2, 1], F32, name="lb", tag="lb")
+            nc.gpsimd.tensor_tensor(out=lb[:], in0=nm[:], in1=rs[:], op=ALU.mult)
+            ln_scale[pr] = rs
+            ln_bias[pr] = lb
+
+        def apply(pr):
+            h, half = divmod(pr, 2)
+            if half == 0:
+                ob = op.tile([P, QB, D], F32, name="ob", tag="ob")
+                o_sb[h] = ob
+            for j in range(2):
+                nc.scalar.activation(
+                    out=o_sb[h][:, 2 * half + j, :], in_=o_ps[pr][:, j, :], func=ACT.Identity,
+                    bias=ln_bias[pr][:, j, :], scale=ln_scale[pr][:, j, :],
+                )
+            if half == 1:
+                nc.sync.dma_start(out=ov[h].rearrange("(p t) d -> p t d", t=QB), in_=o_sb[h][:])
+
+        def unit_ok(u):
+            return 0 <= u < UNITS
+
+        load(0)
+        load(1)
+        for i in range(-5, UNITS + 6):
+            if (i + 5) % QB == 0 and (i + 5) // QB + 2 < HEADS:
+                load((i + 5) // QB + 2)
+            if unit_ok(i + 1):
+                scores(i + 1)
+            if unit_ok(i - 1):
+                recip(i - 1)
+                scale2(i - 1)
+            if (i - 3) % 2 == 1 and unit_ok(i - 3):
+                attn_quant((i - 3) // 2)
+                product((i - 3) // 2)
+            if unit_ok(i + 1):
+                row_max(i + 1)
+            if unit_ok(i):
+                exps(i)
+            if unit_ok(i - 1):
+                combine(i - 1)
+            flipped = None
+            if (i + 5) % QB == 0 and (i + 5) // QB < HEADS:
+                flipped = ("q", (i + 5) // QB, flip_pe(q_sb[(i + 5) // QB]))
+            if (i + 3) % QB == 0 and (i + 3) // QB < HEADS:
+                flipped = ("k", (i + 3) // QB, flip_pe(k_sb[(i + 3) // QB]))
+            if unit_ok(i - 1):
+                attn_flip(i - 1)
+            if unit_ok(i - 2):
+                attn_out(i - 2)
+            if (i - 5) % 2 == 1 and unit_ok(i - 5):
+                norm_consts((i - 5) // 2)
+                apply((i - 5) // 2)
+            if flipped is not None:
+                if flipped[0] == "q":
+                    qT[flipped[1]] = flip_out(flipped[2], "qT")
+                else:
+                    kT[flipped[1]] = flip_out(flipped[2], "kT")
+            if (i - 4) % 2 == 1 and unit_ok(i - 4):
+                stats((i - 4) // 2)
+            if (i + 2) % QB == 0 and (i + 2) // QB < HEADS:
+                value_quant((i + 2) // QB)

@@ -27,7 +27,7 @@ EPS = 1e-5
 GAIN = 1.0 - 0.8
 FLOPS = HEADS * (2 * 2 * S * S * D2 + 2 * S * S * D)
 
-MANUAL = False
+MANUAL = True
 T_ON_G = True
 
 
@@ -43,10 +43,10 @@ def tile_differentialattention_t_kernel(tc, query, key, value, lambda_params, ou
         ld = ctx.enter_context(tc.tile_pool(name="ld", bufs=4))
         tsb = ctx.enter_context(tc.tile_pool(name="tsb", bufs=3))
         vq = ctx.enter_context(tc.tile_pool(name="vq", bufs=3))
-        ep = ctx.enter_context(tc.tile_pool(name="ep", bufs=4))
+        ep = ctx.enter_context(tc.tile_pool(name="ep", bufs=5))
         ap = ctx.enter_context(tc.tile_pool(name="ap", bufs=4))
         gp = ctx.enter_context(tc.tile_pool(name="gp", bufs=3))
-        sm = ctx.enter_context(tc.tile_pool(name="sm", bufs=6))
+        sm = ctx.enter_context(tc.tile_pool(name="sm", bufs=8))
         op = ctx.enter_context(tc.tile_pool(name="op", bufs=3))
         ps_s = ctx.enter_context(tc.psum_pool(name="ps_s", bufs=4))
         ps_t = ctx.enter_context(tc.psum_pool(name="ps_t", bufs=2))
@@ -137,22 +137,24 @@ def tile_differentialattention_t_kernel(tc, query, key, value, lambda_params, ou
                 s_ps[(u, hf)] = sp
 
         def row_max(u):
-            mx = sm.tile([P, 2], F32, name="mx", tag="mx")
-            for hf in range(2):
-                nc.vector.tensor_reduce(out=mx[:, hf:hf + 1], in_=s_ps[(u, hf)][:], axis=AX.X, op=ALU.max)
             nb = sm.tile([P, 2], F32, name="nb", tag="nb")
-            nc.vector.tensor_scalar(out=nb[:], in0=mx[:], scalar1=-SCALE, scalar2=None, op0=ALU.mult)
+            for hf in range(2):
+                x = ep.tile([P, S], F32, name="x", tag="e%d" % hf)
+                nc.vector.tensor_scalar(
+                    out=x[:], in0=s_ps[(u, hf)][:], scalar1=-SCALE, scalar2=None,
+                    op0=ALU.mult, op1=ALU.min, accum_out=nb[:, hf:hf + 1],
+                )
+                e_sb[(u, hf)] = x
             nbias[u] = nb
 
         def exps(u):
             su = sm.tile([P, 2], F32, name="su", tag="su")
             for hf in range(2):
-                e = ep.tile([P, S], F32, name="e", tag="e%d" % hf)
+                e = e_sb[(u, hf)]
                 nc.scalar.activation(
-                    out=e[:], in_=s_ps[(u, hf)][:], func=ACT.Exp,
-                    bias=nbias[u][:, hf:hf + 1], scale=SCALE, accum_out=su[:, hf:hf + 1],
+                    out=e[:], in_=e[:], func=ACT.Exp,
+                    bias=nbias[u][:, hf:hf + 1], scale=-1.0, accum_out=su[:, hf:hf + 1],
                 )
-                e_sb[(u, hf)] = e
             sums[u] = su
 
         def recip(u):
@@ -255,43 +257,61 @@ def tile_differentialattention_t_kernel(tc, query, key, value, lambda_params, ou
         def unit_ok(u):
             return 0 <= u < UNITS
 
+        def head_due(i, off):
+            if (i - off) % QB == 0 and 0 <= (i - off) // QB < HEADS:
+                return (i - off) // QB
+            return -1
+
+        def pair_due(i, lag):
+            if (i - lag) % 2 == 1 and unit_ok(i - lag):
+                return (i - lag) // 2
+            return -1
+
         load(0)
         load(1)
-        for i in range(-5, UNITS + 6):
-            if (i + 5) % QB == 0 and (i + 5) // QB + 2 < HEADS:
-                load((i + 5) // QB + 2)
-            if unit_ok(i + 1):
-                scores(i + 1)
+        for i in range(-8, UNITS + 8):
+            h = head_due(i, -16)
+            if h >= 2:
+                load(h)
+            if unit_ok(i + 2):
+                scores(i + 2)
             if unit_ok(i - 1):
                 recip(i - 1)
                 scale2(i - 1)
-            if (i - 3) % 2 == 1 and unit_ok(i - 3):
-                attn_quant((i - 3) // 2)
-                product((i - 3) // 2)
+            pr = pair_due(i, 5)
+            if pr >= 0:
+                norm_consts(pr)
+            if unit_ok(i - 2):
+                attn_flip(i - 2)
+            hq = head_due(i, -7)
+            hk = head_due(i, -5)
+            flipped = None
+            if hq >= 0:
+                flipped = flip_pe(q_sb[hq])
+            if hk >= 0:
+                flipped = flip_pe(k_sb[hk])
+            pr = pair_due(i, 3)
+            if pr >= 0:
+                attn_quant(pr)
+                product(pr)
             if unit_ok(i + 1):
                 row_max(i + 1)
             if unit_ok(i):
                 exps(i)
             if unit_ok(i - 1):
                 combine(i - 1)
-            flipped = None
-            if (i + 5) % QB == 0 and (i + 5) // QB < HEADS:
-                flipped = ("q", (i + 5) // QB, flip_pe(q_sb[(i + 5) // QB]))
-            if (i + 3) % QB == 0 and (i + 3) // QB < HEADS:
-                flipped = ("k", (i + 3) // QB, flip_pe(k_sb[(i + 3) // QB]))
-            if unit_ok(i - 1):
-                attn_flip(i - 1)
             if unit_ok(i - 2):
                 attn_out(i - 2)
-            if (i - 5) % 2 == 1 and unit_ok(i - 5):
-                norm_consts((i - 5) // 2)
-                apply((i - 5) // 2)
-            if flipped is not None:
-                if flipped[0] == "q":
-                    qT[flipped[1]] = flip_out(flipped[2], "qT")
-                else:
-                    kT[flipped[1]] = flip_out(flipped[2], "kT")
-            if (i - 4) % 2 == 1 and unit_ok(i - 4):
-                stats((i - 4) // 2)
-            if (i + 2) % QB == 0 and (i + 2) // QB < HEADS:
-                value_quant((i + 2) // QB)
+            pr = pair_due(i, 6)
+            if pr >= 0:
+                apply(pr)
+            if hq >= 0:
+                qT[hq] = flip_out(flipped, "qT")
+            if hk >= 0:
+                kT[hk] = flip_out(flipped, "kT")
+            pr = pair_due(i, 4)
+            if pr >= 0:
+                stats(pr)
+            h = head_due(i, -2)
+            if h >= 0:
+                value_quant(h)

@@ -28,7 +28,7 @@ GAIN = 1.0 - 0.8
 FLOPS = HEADS * (2 * 2 * S * S * D2 + 2 * S * S * D)
 
 MANUAL = True
-T_ON_G = True
+T_ON_G = False
 
 
 def tile_differentialattention_t_kernel(tc, query, key, value, lambda_params, out):

@@ -28,7 +28,8 @@ GAIN = 1.0 - 0.8
 FLOPS = HEADS * (2 * 2 * S * S * D2 + 2 * S * S * D)
 
 MANUAL = True
-T_ON_G = False
+T_ON_G = True
+AEV_MOD = 4
 
 
 def tile_differentialattention_t_kernel(tc, query, key, value, lambda_params, out):
@@ -43,11 +44,10 @@ def tile_differentialattention_t_kernel(tc, query, key, value, lambda_params, ou
         ld = ctx.enter_context(tc.tile_pool(name="ld", bufs=4))
         tsb = ctx.enter_context(tc.tile_pool(name="tsb", bufs=3))
         vq = ctx.enter_context(tc.tile_pool(name="vq", bufs=3))
-        ep = ctx.enter_context(tc.tile_pool(name="ep", bufs=5))
-        ap = ctx.enter_context(tc.tile_pool(name="ap", bufs=4))
+        ep = ctx.enter_context(tc.tile_pool(name="ep", bufs=6))
         gp = ctx.enter_context(tc.tile_pool(name="gp", bufs=3))
         sm = ctx.enter_context(tc.tile_pool(name="sm", bufs=8))
-        op = ctx.enter_context(tc.tile_pool(name="op", bufs=3))
+        op = ctx.enter_context(tc.tile_pool(name="op", bufs=4))
         ps_s = ctx.enter_context(tc.psum_pool(name="ps_s", bufs=4))
         ps_t = ctx.enter_context(tc.psum_pool(name="ps_t", bufs=2))
         ps_o = ctx.enter_context(tc.psum_pool(name="ps_o", bufs=2))
@@ -58,6 +58,10 @@ def tile_differentialattention_t_kernel(tc, query, key, value, lambda_params, ou
         nc.sync.dma_start(out=lam_bf[:], in_=lambda_params.partition_broadcast(P))
         lam = const.tile([P, 2], F32, name="lam")
         nc.vector.tensor_copy(out=lam[:], in_=lam_bf[:])
+        nlam = const.tile([P, 2], F32, name="nlam")
+        nc.vector.tensor_scalar(out=nlam[:], in0=lam[:], scalar1=-1.0, scalar2=None, op0=ALU.mult)
+        ident_f = const.tile([P, P], F32, name="ident_f")
+        make_identity(nc, ident_f[:])
         neghalf = const.tile([P, 2, 1], F32, name="neghalf")
         nc.gpsimd.memset(neghalf[:], -0.5)
 
@@ -76,14 +80,13 @@ def tile_differentialattention_t_kernel(tc, query, key, value, lambda_params, ou
         sums = {}
         rec = {}
         e_sb = {}
-        attn = {}
         aT = {}
         grp = {}
         a_codes = {}
         a_scales = {}
         o_ps = {}
         mv = {}
-        ln_scale = {}
+        ssq = {}
         ln_bias = {}
         o_sb = {}
 
@@ -167,22 +170,24 @@ def tile_differentialattention_t_kernel(tc, query, key, value, lambda_params, ou
             eng = nc.gpsimd if T_ON_G else nc.vector
             e2 = e_sb[(u, 1)]
             eng.tensor_scalar(
-                out=e2[:], in0=e2[:], scalar1=rec[u][:, 1:2], scalar2=lam[:, (h % 2):(h % 2) + 1],
+                out=e2[:], in0=e2[:], scalar1=rec[u][:, 1:2], scalar2=nlam[:, (h % 2):(h % 2) + 1],
                 op0=ALU.mult, op1=ALU.mult,
             )
 
         def combine(u):
-            at = ap.tile([P, S], BF16, name="at", tag="at")
-            nc.vector.scalar_tensor_tensor(
-                out=at[:], in0=e_sb[(u, 0)][:], scalar=rec[u][:, 0:1], in1=e_sb[(u, 1)][:],
-                op0=ALU.mult, op1=ALU.subtract,
+            e1 = e_sb[(u, 0)]
+            nc.vector.tensor_scalar(
+                out=e1[:], in0=e1[:], scalar1=rec[u][:, 0:1], scalar2=None, op0=ALU.mult
             )
-            attn[u] = at
 
         def attn_flip(u):
-            tp = ps_t.tile([P, QB, P], BF16, name="tpa", tag="tr")
+            tp = ps_t.tile([P, QB, P], F32, name="tpa", tag="tr")
             for t in range(QB):
-                nc.tensor.transpose(tp[:, t, :], attn[u][:, t * P:(t + 1) * P], ident[:])
+                for hf in range(2):
+                    nc.tensor.matmul(
+                        tp[:, t, :], lhsT=e_sb[(u, hf)][:, t * P:(t + 1) * P], rhs=ident_f[:],
+                        is_transpose=True, start=(hf == 0), stop=(hf == 1),
+                    )
             aT[u] = tp
 
         def attn_out(u):
@@ -190,7 +195,10 @@ def tile_differentialattention_t_kernel(tc, query, key, value, lambda_params, ou
             if j == 0:
                 g = gp.tile([P, 2, P, 4], BF16, name="g", tag="g", align_bytes=64)
                 grp[pr] = g
-            nc.scalar.copy(out=grp[pr][:, j, :, :], in_=aT[u][:].rearrange("p t q -> p q t"))
+            if u % AEV_MOD == 1:
+                nc.vector.tensor_copy(out=grp[pr][:, j, :, :], in_=aT[u][:].rearrange("p t q -> p q t"))
+            else:
+                nc.scalar.copy(out=grp[pr][:, j, :, :], in_=aT[u][:].rearrange("p t q -> p q t"))
 
         def attn_quant(pr):
             ac = gp.tile([P, 2 * P], U32, name="ac", tag="ac", align_bytes=64)
@@ -215,44 +223,51 @@ def tile_differentialattention_t_kernel(tc, query, key, value, lambda_params, ou
                 )
             o_ps[pr] = o
 
-        def stats(pr):
-            st = sm.tile([P, 2, 6], F32, name="st", tag="st")
-            m = sm.tile([P, 2, 2], F32, name="m", tag="m")
+        def ln_sum(pr):
+            ob = op.tile([P, 2, D], F32, name="ob", tag="ob")
+            ls = sm.tile([P, 2, 1], F32, name="ls", tag="ls")
             for j in range(2):
-                nc.vector.bn_stats(out=st[:, j, :], in_=o_ps[pr][:, j, :])
-            for j in range(2):
-                nc.vector.bn_aggr(out=m[:, j, :], in_=st[:, j, :])
-            mv[pr] = m
+                nc.scalar.activation(
+                    out=ob[:, j, :], in_=o_ps[pr][:, j, :], func=ACT.Identity, accum_out=ls[:, j, :]
+                )
+            o_sb[pr] = ob
+            mv[pr] = ls
 
-        def norm_consts(pr):
-            a = sm.tile([P, 2, 1], F32, name="a", tag="a")
-            nc.gpsimd.tensor_scalar(
-                out=a[:], in0=mv[pr][:, :, 1:2], scalar1=1.0 / (GAIN * GAIN), scalar2=EPS / (GAIN * GAIN),
-                op0=ALU.mult, op1=ALU.add,
-            )
+        def ln_mean(pr):
             nm = sm.tile([P, 2, 1], F32, name="nm", tag="nm")
             nc.gpsimd.tensor_scalar(
-                out=nm[:], in0=mv[pr][:, :, 0:1], scalar1=-1.0, scalar2=0.0, op0=ALU.mult, op1=ALU.add
+                out=nm[:], in0=mv[pr][:], scalar1=-1.0 / D, scalar2=0.0, op0=ALU.mult, op1=ALU.add
+            )
+            ln_bias[pr] = nm
+
+        def ln_square(pr):
+            sq = sm.tile([P, 2, 1], F32, name="sq", tag="sq")
+            for j in range(2):
+                junk = op.tile([P, D], BF16, name="junk", tag="junk")
+                nc.scalar.activation(
+                    out=junk[:], in_=o_sb[pr][:, j, :], func=ACT.Square,
+                    bias=ln_bias[pr][:, j, :], scale=1.0, accum_out=sq[:, j, :],
+                )
+            ssq[pr] = sq
+
+        def ln_apply(pr):
+            h, half = divmod(pr, 2)
+            a = sm.tile([P, 2, 1], F32, name="a", tag="a")
+            nc.gpsimd.tensor_scalar(
+                out=a[:], in0=ssq[pr][:], scalar1=1.0 / (D * GAIN * GAIN), scalar2=EPS / (GAIN * GAIN),
+                op0=ALU.mult, op1=ALU.add,
             )
             rs = sm.tile([P, 2, 1], F32, name="rs", tag="rs")
             nc.gpsimd.tensor_tensor(out=rs[:], in0=a[:], in1=neghalf[:], op=ALU.pow)
-            lb = sm.tile([P, 2, 1], F32, name="lb", tag="lb")
-            nc.gpsimd.tensor_tensor(out=lb[:], in0=nm[:], in1=rs[:], op=ALU.mult)
-            ln_scale[pr] = rs
-            ln_bias[pr] = lb
-
-        def apply(pr):
-            h, half = divmod(pr, 2)
-            if half == 0:
-                ob = op.tile([P, QB, D], F32, name="ob", tag="ob")
-                o_sb[h] = ob
+            ob = o_sb[pr]
             for j in range(2):
-                nc.scalar.activation(
-                    out=o_sb[h][:, 2 * half + j, :], in_=o_ps[pr][:, j, :], func=ACT.Identity,
-                    bias=ln_bias[pr][:, j, :], scale=ln_scale[pr][:, j, :],
+                nc.gpsimd.tensor_scalar(
+                    out=ob[:, j, :], in0=ob[:, j, :], scalar1=ln_bias[pr][:, j, :], scalar2=rs[:, j, :],
+                    op0=ALU.add, op1=ALU.mult,
                 )
-            if half == 1:
-                nc.sync.dma_start(out=ov[h].rearrange("(p t) d -> p t d", t=QB), in_=o_sb[h][:])
+            nc.sync.dma_start(
+                out=ov[h].rearrange("(p t) d -> p t d", t=QB)[:, 2 * half:2 * half + 2, :], in_=ob[:]
+            )
 
         def unit_ok(u):
             return 0 <= u < UNITS
@@ -269,22 +284,26 @@ def tile_differentialattention_t_kernel(tc, query, key, value, lambda_params, ou
 
         load(0)
         load(1)
-        for i in range(-8, UNITS + 8):
-            h = head_due(i, -16)
+        for i in range(-9, UNITS + 9):
+            h = head_due(i, -17)
             if h >= 2:
                 load(h)
             if unit_ok(i + 2):
                 scores(i + 2)
             if unit_ok(i - 1):
                 recip(i - 1)
+                combine(i - 1)
                 scale2(i - 1)
             pr = pair_due(i, 5)
             if pr >= 0:
-                norm_consts(pr)
+                ln_mean(pr)
+            pr = pair_due(i, 7)
+            if pr >= 0:
+                ln_apply(pr)
             if unit_ok(i - 2):
                 attn_flip(i - 2)
-            hq = head_due(i, -7)
-            hk = head_due(i, -5)
+            hq = head_due(i, -8)
+            hk = head_due(i, -6)
             flipped = None
             if hq >= 0:
                 flipped = flip_pe(q_sb[hq])
@@ -298,20 +317,18 @@ def tile_differentialattention_t_kernel(tc, query, key, value, lambda_params, ou
                 row_max(i + 1)
             if unit_ok(i):
                 exps(i)
-            if unit_ok(i - 1):
-                combine(i - 1)
             if unit_ok(i - 2):
                 attn_out(i - 2)
+            pr = pair_due(i, 4)
+            if pr >= 0:
+                ln_sum(pr)
             pr = pair_due(i, 6)
             if pr >= 0:
-                apply(pr)
+                ln_square(pr)
             if hq >= 0:
                 qT[hq] = flip_out(flipped, "qT")
             if hk >= 0:
                 kT[hk] = flip_out(flipped, "kT")
-            pr = pair_due(i, 4)
-            if pr >= 0:
-                stats(pr)
-            h = head_due(i, -2)
+            h = head_due(i, -3)
             if h >= 0:
                 value_quant(h)

@@ -292,7 +292,6 @@ def tile_differentialattention_t_kernel(tc, query, key, value, lambda_params, ou
                 scores(i + 2)
             if unit_ok(i - 1):
                 recip(i - 1)
-                combine(i - 1)
                 scale2(i - 1)
             pr = pair_due(i, 5)
             if pr >= 0:
@@ -309,12 +308,14 @@ def tile_differentialattention_t_kernel(tc, query, key, value, lambda_params, ou
                 flipped = flip_pe(q_sb[hq])
             if hk >= 0:
                 flipped = flip_pe(k_sb[hk])
+            if unit_ok(i + 1):
+                row_max(i + 1)
             pr = pair_due(i, 3)
             if pr >= 0:
                 attn_quant(pr)
                 product(pr)
-            if unit_ok(i + 1):
-                row_max(i + 1)
+            if unit_ok(i - 1):
+                combine(i - 1)
             if unit_ok(i):
                 exps(i)
             if unit_ok(i - 2):

@@ -1,9 +1,7 @@
 from contextlib import ExitStack
 import math
 
-import concourse.bass as bass
 import concourse.mybir as mybir
-import concourse.tile as tile
 from concourse.masks import make_identity
 
 F32 = mybir.dt.float32
@@ -22,14 +20,11 @@ D = 256
 D2 = 128
 QB = 4
 UNITS = HEADS * QB
+PAIRS = UNITS // 2
 SCALE = 1.0 / math.sqrt(D2)
 EPS = 1e-5
 GAIN = 1.0 - 0.8
 FLOPS = HEADS * (2 * 2 * S * S * D2 + 2 * S * S * D)
-
-MANUAL = True
-T_ON_G = True
-AEV_MOD = 4
 
 
 def tile_differentialattention_t_kernel(tc, query, key, value, lambda_params, out):
@@ -56,23 +51,21 @@ def tile_differentialattention_t_kernel(tc, query, key, value, lambda_params, ou
         make_identity(nc, ident[:])
         lam_bf = const.tile([P, 2], BF16, name="lam_bf")
         nc.sync.dma_start(out=lam_bf[:], in_=lambda_params.partition_broadcast(P))
-        lam = const.tile([P, 2], F32, name="lam")
-        nc.vector.tensor_copy(out=lam[:], in_=lam_bf[:])
         nlam = const.tile([P, 2], F32, name="nlam")
-        nc.vector.tensor_scalar(out=nlam[:], in0=lam[:], scalar1=-1.0, scalar2=None, op0=ALU.mult)
+        nc.vector.tensor_scalar(out=nlam[:], in0=lam_bf[:], scalar1=-1.0, scalar2=None, op0=ALU.mult)
         ident_f = const.tile([P, P], F32, name="ident_f")
         make_identity(nc, ident_f[:])
         neghalf = const.tile([P, 2, 1], F32, name="neghalf")
         nc.gpsimd.memset(neghalf[:], -0.5)
 
-        if MANUAL:
-            ctx.enter_context(tc.manual_schedule())
+        ctx.enter_context(tc.manual_schedule())
 
         q_sb = {}
         k_sb = {}
         v_sb = {}
         qT = {}
         kT = {}
+        v_grp = {}
         v_codes = {}
         v_scales = {}
         s_ps = {}
@@ -86,19 +79,20 @@ def tile_differentialattention_t_kernel(tc, query, key, value, lambda_params, ou
         a_scales = {}
         o_ps = {}
         mv = {}
-        ssq = {}
+        ln_scale = {}
         ln_bias = {}
-        o_sb = {}
 
-        def load(h):
+        def load_qk(h):
             tq = ld.tile([P, QB, D], BF16, name="tq", tag="q")
             nc.sync.dma_start(out=tq[:], in_=qv[h].rearrange("(p t) d -> p t d", t=QB))
             tk = ld.tile([P, QB, D], BF16, name="tk", tag="k")
             nc.sync.dma_start(out=tk[:], in_=kv[h].rearrange("(t p) d -> p t d", p=P))
-            tv = ld.tile([P, QB, D], BF16, name="tv", tag="v")
-            nc.sync.dma_start(out=tv[:], in_=vv[h].rearrange("(t p) d -> p t d", p=P))
             q_sb[h] = tq
             k_sb[h] = tk
+
+        def load_v(h):
+            tv = ld.tile([P, QB, D], BF16, name="tv", tag="v")
+            nc.sync.dma_start(out=tv[:], in_=vv[h].rearrange("(t p) d -> p t d", p=P))
             v_sb[h] = tv
 
         def flip_pe(src):
@@ -115,19 +109,27 @@ def tile_differentialattention_t_kernel(tc, query, key, value, lambda_params, ou
             nc.scalar.copy(out=dst[:], in_=tp[:])
             return dst
 
-        def value_quant(h):
-            vg = vq.tile([P, D, 4], BF16, name="vg", tag="vg", align_bytes=64)
+        def value_group(h, half):
+            if half == 0:
+                vg = vq.tile([P, D, 4], BF16, name="vg", tag="vg", align_bytes=64)
+                v_grp[h] = vg
+            cols = slice(half * P, (half + 1) * P)
             nc.vector.tensor_copy(
-                out=vg[:].rearrange("p (c i) t -> p c t i", i=4),
-                in_=v_sb[h][:].rearrange("p t (c i) -> p c t i", i=4),
+                out=v_grp[h][:, cols, :].rearrange("p (c i) t -> p c t i", i=4),
+                in_=v_sb[h][:, :, cols].rearrange("p t (c i) -> p c t i", i=4),
             )
-            vc = vq.tile([P, D], U32, name="vc", tag="vc", align_bytes=64)
-            vs = vq.tile([P, D], U8, name="vs", tag="vs", align_bytes=64)
+
+        def value_quant(h, half):
+            if half == 0:
+                vc = vq.tile([P, D], U32, name="vc", tag="vc", align_bytes=64)
+                vs = vq.tile([P, D], U8, name="vs", tag="vs", align_bytes=64)
+                v_codes[h] = vc
+                v_scales[h] = vs
+            cols = slice(half * P, (half + 1) * P)
             nc.vector.quantize_mx(
-                out=vc[:].bitcast(FP8X4), scales=vs[:], in_=vg[:].rearrange("p f t -> p (f t)")
+                out=v_codes[h][:, cols].bitcast(FP8X4), scales=v_scales[h][:, cols],
+                in_=v_grp[h][:, cols, :].rearrange("p f t -> p (f t)"),
             )
-            v_codes[h] = vc
-            v_scales[h] = vs
 
         def scores(u):
             h, t = divmod(u, QB)
@@ -167,9 +169,8 @@ def tile_differentialattention_t_kernel(tc, query, key, value, lambda_params, ou
 
         def scale2(u):
             h = u // QB
-            eng = nc.gpsimd if T_ON_G else nc.vector
             e2 = e_sb[(u, 1)]
-            eng.tensor_scalar(
+            nc.gpsimd.tensor_scalar(
                 out=e2[:], in0=e2[:], scalar1=rec[u][:, 1:2], scalar2=nlam[:, (h % 2):(h % 2) + 1],
                 op0=ALU.mult, op1=ALU.mult,
             )
@@ -195,16 +196,14 @@ def tile_differentialattention_t_kernel(tc, query, key, value, lambda_params, ou
             if j == 0:
                 g = gp.tile([P, 2, P, 4], BF16, name="g", tag="g", align_bytes=64)
                 grp[pr] = g
-            if u % AEV_MOD == 1:
-                nc.vector.tensor_copy(out=grp[pr][:, j, :, :], in_=aT[u][:].rearrange("p t q -> p q t"))
-            else:
-                nc.scalar.copy(out=grp[pr][:, j, :, :], in_=aT[u][:].rearrange("p t q -> p q t"))
+            nc.scalar.copy(out=grp[pr][:, j, :, :], in_=aT[u][:].rearrange("p t q -> p q t"))
 
         def attn_quant(pr):
             ac = gp.tile([P, 2 * P], U32, name="ac", tag="ac", align_bytes=64)
             asc = gp.tile([P, 2 * P], U8, name="asc", tag="asc", align_bytes=64)
             nc.vector.quantize_mx(
-                out=ac[:].bitcast(FP8X4), scales=asc[:], in_=grp[pr][:].rearrange("p j q t -> p (j q t)")
+                out=ac[:].bitcast(FP8X4), scales=asc[:],
+                in_=grp[pr][:].rearrange("p j q t -> p (j q t)"),
             )
             a_codes[pr] = ac
             a_scales[pr] = asc
@@ -223,47 +222,41 @@ def tile_differentialattention_t_kernel(tc, query, key, value, lambda_params, ou
                 )
             o_ps[pr] = o
 
-        def ln_sum(pr):
-            ob = op.tile([P, 2, D], F32, name="ob", tag="ob")
-            ls = sm.tile([P, 2, 1], F32, name="ls", tag="ls")
+        def ln_stats(pr):
+            st = sm.tile([P, 2, 6], F32, name="st", tag="st")
+            m = sm.tile([P, 2, 2], F32, name="m", tag="m")
             for j in range(2):
-                nc.scalar.activation(
-                    out=ob[:, j, :], in_=o_ps[pr][:, j, :], func=ACT.Identity, accum_out=ls[:, j, :]
-                )
-            o_sb[pr] = ob
-            mv[pr] = ls
-
-        def ln_mean(pr):
-            nm = sm.tile([P, 2, 1], F32, name="nm", tag="nm")
-            nc.gpsimd.tensor_scalar(
-                out=nm[:], in0=mv[pr][:], scalar1=-1.0 / D, scalar2=0.0, op0=ALU.mult, op1=ALU.add
-            )
-            ln_bias[pr] = nm
-
-        def ln_square(pr):
-            sq = sm.tile([P, 2, 1], F32, name="sq", tag="sq")
+                nc.vector.bn_stats(out=st[:, j, :], in_=o_ps[pr][:, j, :])
             for j in range(2):
-                junk = op.tile([P, D], BF16, name="junk", tag="junk")
-                nc.scalar.activation(
-                    out=junk[:], in_=o_sb[pr][:, j, :], func=ACT.Square,
-                    bias=ln_bias[pr][:, j, :], scale=1.0, accum_out=sq[:, j, :],
-                )
-            ssq[pr] = sq
+                nc.vector.bn_aggr(out=m[:, j, :], in_=st[:, j, :])
+            mv[pr] = m
 
-        def ln_apply(pr):
-            h, half = divmod(pr, 2)
+        def ln_coeffs(pr):
+            m = mv[pr]
             a = sm.tile([P, 2, 1], F32, name="a", tag="a")
             nc.gpsimd.tensor_scalar(
-                out=a[:], in0=ssq[pr][:], scalar1=1.0 / (D * GAIN * GAIN), scalar2=EPS / (GAIN * GAIN),
+                out=a[:], in0=m[:, :, 1:2], scalar1=1.0 / (GAIN * GAIN), scalar2=EPS / (GAIN * GAIN),
                 op0=ALU.mult, op1=ALU.add,
             )
             rs = sm.tile([P, 2, 1], F32, name="rs", tag="rs")
             nc.gpsimd.tensor_tensor(out=rs[:], in0=a[:], in1=neghalf[:], op=ALU.pow)
-            ob = o_sb[pr]
+            ln_scale[pr] = rs
+
+        def ln_shift(pr):
+            lb = sm.tile([P, 2, 1], F32, name="lb", tag="lb")
+            nc.vector.scalar_tensor_tensor(
+                out=lb[:], in0=mv[pr][:, :, 0:1], scalar=-1.0, in1=ln_scale[pr][:],
+                op0=ALU.mult, op1=ALU.mult,
+            )
+            ln_bias[pr] = lb
+
+        def ln_apply(pr):
+            h, half = divmod(pr, 2)
+            ob = op.tile([P, 2, D], F32, name="ob", tag="ob")
             for j in range(2):
-                nc.gpsimd.tensor_scalar(
-                    out=ob[:, j, :], in0=ob[:, j, :], scalar1=ln_bias[pr][:, j, :], scalar2=rs[:, j, :],
-                    op0=ALU.add, op1=ALU.mult,
+                nc.scalar.activation(
+                    out=ob[:, j, :], in_=o_ps[pr][:, j, :], func=ACT.Identity,
+                    bias=ln_bias[pr][:, j, :], scale=ln_scale[pr][:, j, :],
                 )
             nc.sync.dma_start(
                 out=ov[h].rearrange("(p t) d -> p t d", t=QB)[:, 2 * half:2 * half + 2, :], in_=ob[:]
@@ -278,58 +271,75 @@ def tile_differentialattention_t_kernel(tc, query, key, value, lambda_params, ou
             return -1
 
         def pair_due(i, lag):
-            if (i - lag) % 2 == 1 and unit_ok(i - lag):
+            if (i - lag) % 2 == 0 and 0 <= (i - lag) // 2 < PAIRS:
                 return (i - lag) // 2
             return -1
 
-        load(0)
-        load(1)
-        for i in range(-9, UNITS + 9):
-            h = head_due(i, -17)
+        load_qk(0)
+        load_qk(1)
+        load_v(0)
+        for i in range(-7, UNITS + 10):
+            h = head_due(i, -11)
             if h >= 2:
-                load(h)
-            if unit_ok(i + 2):
-                scores(i + 2)
-            if unit_ok(i - 1):
-                recip(i - 1)
-                scale2(i - 1)
-            pr = pair_due(i, 5)
-            if pr >= 0:
-                ln_mean(pr)
-            pr = pair_due(i, 7)
+                load_qk(h)
+            h = head_due(i, -11)
+            if h >= 1:
+                load_v(h)
+
+            if unit_ok(i - 2):
+                recip(i - 2)
+                scale2(i - 2)
+            if unit_ok(i):
+                row_max(i)
+            pr = pair_due(i, 9)
             if pr >= 0:
                 ln_apply(pr)
-            if unit_ok(i - 2):
-                attn_flip(i - 2)
-            hq = head_due(i, -8)
-            hk = head_due(i, -6)
+            if unit_ok(i + 1):
+                scores(i + 1)
+            pr = pair_due(i, 6)
+            if pr >= 0:
+                ln_stats(pr)
+            if unit_ok(i - 3):
+                attn_flip(i - 3)
+            pr = pair_due(i, 7)
+            if pr >= 0:
+                ln_coeffs(pr)
+            pr = pair_due(i, 8)
+            if pr >= 0:
+                ln_shift(pr)
+            if unit_ok(i):
+                exps(i)
+            hq = head_due(i, -6)
+            hk = head_due(i, -4)
             flipped = None
             if hq >= 0:
                 flipped = flip_pe(q_sb[hq])
             if hk >= 0:
                 flipped = flip_pe(k_sb[hk])
-            if unit_ok(i + 1):
-                row_max(i + 1)
-            pr = pair_due(i, 3)
+
+            h = head_due(i, 1)
+            if h >= 0:
+                value_quant(h, 1)
+            h = head_due(i, -1)
+            if h >= 0:
+                value_quant(h, 0)
+            pr = pair_due(i, 5)
             if pr >= 0:
                 attn_quant(pr)
-                product(pr)
-            if unit_ok(i - 1):
-                combine(i - 1)
-            if unit_ok(i):
-                exps(i)
+            h = head_due(i, -2)
+            if h >= 0:
+                value_group(h, 1)
             if unit_ok(i - 2):
-                attn_out(i - 2)
-            pr = pair_due(i, 4)
-            if pr >= 0:
-                ln_sum(pr)
-            pr = pair_due(i, 6)
-            if pr >= 0:
-                ln_square(pr)
+                combine(i - 2)
+            h = head_due(i, -5)
+            if h >= 0:
+                value_group(h, 0)
+
+            if unit_ok(i - 3):
+                attn_out(i - 3)
             if hq >= 0:
                 qT[hq] = flip_out(flipped, "qT")
             if hk >= 0:
                 kT[hk] = flip_out(flipped, "kT")
-            h = head_due(i, -3)
-            if h >= 0:
-                value_quant(h)
+            if pr >= 0:
+                product(pr)

@@ -223,19 +223,15 @@ def tile_differentialattention_t_kernel(tc, query, key, value, lambda_params, ou
             o_ps[pr] = o
 
         def ln_stats(pr):
-            st = sm.tile([P, 2, 6], F32, name="st", tag="st")
-            m = sm.tile([P, 2, 2], F32, name="m", tag="m")
-            for j in range(2):
-                nc.vector.bn_stats(out=st[:, j, :], in_=o_ps[pr][:, j, :])
-            for j in range(2):
-                nc.vector.bn_aggr(out=m[:, j, :], in_=st[:, j, :])
-            mv[pr] = m
+            st = sm.tile([P, 6], F32, name="st", tag="st")
+            nc.vector.bn_stats(out=st[:], in_=o_ps[pr][:].rearrange("p j d -> p d j"))
+            mv[pr] = st[:].rearrange("p (j s) -> p j s", s=3)
 
         def ln_coeffs(pr):
             m = mv[pr]
             a = sm.tile([P, 2, 1], F32, name="a", tag="a")
             nc.gpsimd.tensor_scalar(
-                out=a[:], in0=m[:, :, 1:2], scalar1=1.0 / (GAIN * GAIN), scalar2=EPS / (GAIN * GAIN),
+                out=a[:], in0=m[:, :, 2:3], scalar1=1.0 / (D * GAIN * GAIN), scalar2=EPS / (GAIN * GAIN),
                 op0=ALU.mult, op1=ALU.add,
             )
             rs = sm.tile([P, 2, 1], F32, name="rs", tag="rs")
@@ -245,7 +241,7 @@ def tile_differentialattention_t_kernel(tc, query, key, value, lambda_params, ou
         def ln_shift(pr):
             lb = sm.tile([P, 2, 1], F32, name="lb", tag="lb")
             nc.vector.scalar_tensor_tensor(
-                out=lb[:], in0=mv[pr][:, :, 0:1], scalar=-1.0, in1=ln_scale[pr][:],
+                out=lb[:], in0=mv[pr][:, :, 1:2], scalar=-1.0, in1=ln_scale[pr][:],
                 op0=ALU.mult, op1=ALU.mult,
             )
             ln_bias[pr] = lb

@@ -47,12 +47,10 @@ def tile_differentialattention_t_kernel(tc, query, key, value, lambda_params, ou
         ps_t = ctx.enter_context(tc.psum_pool(name="ps_t", bufs=2))
         ps_o = ctx.enter_context(tc.psum_pool(name="ps_o", bufs=2))
 
+        zeros = const.tile([P, S], BF16, name="zeros")
+        nc.vector.memset(zeros[:], 0.0)
         ident = const.tile([P, P], BF16, name="ident")
         make_identity(nc, ident[:])
-        lam_bf = const.tile([P, 2], BF16, name="lam_bf")
-        nc.sync.dma_start(out=lam_bf[:], in_=lambda_params.partition_broadcast(P))
-        nlam = const.tile([P, 2], F32, name="nlam")
-        nc.vector.tensor_scalar(out=nlam[:], in0=lam_bf[:], scalar1=-1.0, scalar2=None, op0=ALU.mult)
         ident_f = const.tile([P, P], F32, name="ident_f")
         make_identity(nc, ident_f[:])
         neghalf = const.tile([P, 2, 1], F32, name="neghalf")
@@ -83,10 +81,10 @@ def tile_differentialattention_t_kernel(tc, query, key, value, lambda_params, ou
         ln_bias = {}
 
         def load_qk(h):
-            tq = ld.tile([P, QB, D], BF16, name="tq", tag="q")
-            nc.sync.dma_start(out=tq[:], in_=qv[h].rearrange("(p t) d -> p t d", t=QB))
             tk = ld.tile([P, QB, D], BF16, name="tk", tag="k")
             nc.sync.dma_start(out=tk[:], in_=kv[h].rearrange("(t p) d -> p t d", p=P))
+            tq = ld.tile([P, QB, D], BF16, name="tq", tag="q")
+            nc.sync.dma_start(out=tq[:], in_=qv[h].rearrange("(p t) d -> p t d", t=QB))
             q_sb[h] = tq
             k_sb[h] = tk
 
@@ -103,6 +101,22 @@ def tile_differentialattention_t_kernel(tc, query, key, value, lambda_params, ou
                         tp[:, hf, t * P:(t + 1) * P], src[:, t, hf * D2:(hf + 1) * D2], ident[:]
                     )
             return tp
+
+        def flip_first():
+            kT[0] = tsb.tile([P, 2, S], BF16, name="dst", tag="kT")
+            qT[0] = tsb.tile([P, 2, S], BF16, name="dst", tag="qT")
+            for hf in range(2):
+                for src, dst, copy in (
+                    (k_sb[0], kT[0], nc.vector.tensor_copy), (q_sb[0], qT[0], nc.scalar.copy)
+                ):
+                    tp = ps_s.tile([P, S], BF16, name="tph", tag="s")
+                    for t in range(QB):
+                        nc.tensor.transpose(
+                            tp[:, t * P:(t + 1) * P], src[:, t, hf * D2:(hf + 1) * D2], ident[:]
+                        )
+                    copy(out=dst[:, hf, :], in_=tp[:])
+                if hf == 0:
+                    value_group(0, 0)
 
         def flip_out(tp, tag):
             dst = tsb.tile([P, 2, S], BF16, name="dst", tag=tag)
@@ -272,14 +286,25 @@ def tile_differentialattention_t_kernel(tc, query, key, value, lambda_params, ou
             return -1
 
         load_qk(0)
-        load_qk(1)
         load_v(0)
-        for i in range(-7, UNITS + 10):
+        lam_bf = const.tile([P, 2], BF16, name="lam_bf")
+        nc.sync.dma_start(out=lam_bf[:], in_=lambda_params.partition_broadcast(P))
+        nlam = const.tile([P, 2], F32, name="nlam")
+        nc.gpsimd.tensor_scalar(
+            out=nlam[:], in0=lam_bf[:], scalar1=-1.0, scalar2=0.0, op0=ALU.mult, op1=ALU.add
+        )
+        for h in range(1, 3):
+            load_qk(h)
+            load_v(h)
+        for w in range(5):
+            wp = ps_t.tile([P, S], F32, name="wp", tag="tr")
+            nc.tensor.matmul(wp[:], lhsT=zeros[:, 0:P], rhs=zeros[:], start=True, stop=True)
+        flip_first()
+        scores(0)
+        for i in range(UNITS + 10):
             h = head_due(i, -11)
-            if h >= 2:
+            if h >= 0:
                 load_qk(h)
-            h = head_due(i, -11)
-            if h >= 1:
                 load_v(h)
 
             if unit_ok(i - 2):
@@ -305,7 +330,7 @@ def tile_differentialattention_t_kernel(tc, query, key, value, lambda_params, ou
                 ln_shift(pr)
             if unit_ok(i):
                 exps(i)
-            hq = head_due(i, -6)
+            hq = 1 if i == 1 else head_due(i, -6)
             hk = head_due(i, -4)
             flipped = None
             if hq >= 0:
@@ -315,21 +340,21 @@ def tile_differentialattention_t_kernel(tc, query, key, value, lambda_params, ou
 
             h = head_due(i, 1)
             if h >= 0:
-                value_quant(h, 1)
-            h = head_due(i, -1)
-            if h >= 0:
                 value_quant(h, 0)
+            h = head_due(i, 3)
+            if h >= 0:
+                value_quant(h, 1)
             pr = pair_due(i, 5)
             if pr >= 0:
                 attn_quant(pr)
-            h = head_due(i, -2)
-            if h >= 0:
-                value_group(h, 1)
             if unit_ok(i - 2):
                 combine(i - 2)
-            h = head_due(i, -5)
-            if h >= 0:
+            h = head_due(i, 0)
+            if h >= 1:
                 value_group(h, 0)
+            h = head_due(i, 2)
+            if h >= 0:
+                value_group(h, 1)
 
             if unit_ok(i - 3):
                 attn_out(i - 3)

@@ -56,6 +56,12 @@ def tile_differentialattention_t_kernel(tc, query, key, value, lambda_params, ou
         neghalf = const.tile([P, 2, 1], F32, name="neghalf")
         nc.gpsimd.memset(neghalf[:], -0.5)
 
+        eps_g = const.tile([P, 2, 1], F32, name="eps_g")
+        nc.gpsimd.tensor_scalar(
+            out=eps_g[:], in0=neghalf[:], scalar1=0.0, scalar2=EPS / (GAIN * GAIN), op0=ALU.mult, op1=ALU.add
+        )
+        sqrt_warm = const.tile([P, 2, 1], F32, name="sqrt_warm")
+
         ctx.enter_context(tc.manual_schedule())
 
         q_sb = {}
@@ -72,6 +78,7 @@ def tile_differentialattention_t_kernel(tc, query, key, value, lambda_params, ou
         rec = {}
         e_sb = {}
         aT = {}
+        d_sb = {}
         grp = {}
         a_codes = {}
         a_scales = {}
@@ -181,10 +188,10 @@ def tile_differentialattention_t_kernel(tc, query, key, value, lambda_params, ou
             nc.vector.reciprocal(out=r[:], in_=sums[u][:])
             rec[u] = r
 
-        def scale2(u):
+        def scale2(u, eng):
             h = u // QB
             e2 = e_sb[(u, 1)]
-            nc.gpsimd.tensor_scalar(
+            eng.tensor_scalar(
                 out=e2[:], in0=e2[:], scalar1=rec[u][:, 1:2], scalar2=nlam[:, (h % 2):(h % 2) + 1],
                 op0=ALU.mult, op1=ALU.mult,
             )
@@ -212,6 +219,32 @@ def tile_differentialattention_t_kernel(tc, query, key, value, lambda_params, ou
                 grp[pr] = g
             nc.scalar.copy(out=grp[pr][:, j, :, :], in_=aT[u][:].rearrange("p t q -> p q t"))
 
+        def attn_round(u):
+            d = op.tile([P, S], BF16, name="d", tag="d")
+            nc.vector.scalar_tensor_tensor(
+                out=d[:], in0=e_sb[(u, 0)][:], scalar=rec[u][:, 0:1], in1=e_sb[(u, 1)][:],
+                op0=ALU.mult, op1=ALU.add,
+            )
+            d_sb[u] = d
+
+        def attn_flip_rounded(u):
+            tp = ps_t.tile([P, QB, P], BF16, name="tpd", tag="tr")
+            for t in range(QB):
+                nc.tensor.transpose(tp[:, t, :], d_sb[u][:, t * P:(t + 1) * P], ident[:])
+            aT[u] = tp
+
+        def attn_quant_half(pr, j):
+            if j == 0:
+                ac = gp.tile([P, 2 * P], U32, name="ac", tag="ac", align_bytes=64)
+                asc = gp.tile([P, 2 * P], U8, name="asc", tag="asc", align_bytes=64)
+                a_codes[pr] = ac
+                a_scales[pr] = asc
+            cols = slice(j * P, (j + 1) * P)
+            nc.vector.quantize_mx(
+                out=a_codes[pr][:, cols].bitcast(FP8X4), scales=a_scales[pr][:, cols],
+                in_=grp[pr][:, j, :, :].rearrange("p q t -> p (q t)"),
+            )
+
         def attn_quant(pr):
             ac = gp.tile([P, 2 * P], U32, name="ac", tag="ac", align_bytes=64)
             asc = gp.tile([P, 2 * P], U8, name="asc", tag="asc", align_bytes=64)
@@ -223,18 +256,23 @@ def tile_differentialattention_t_kernel(tc, query, key, value, lambda_params, ou
             a_scales[pr] = asc
 
         def product(pr):
-            h = pr // 2
-            o = ps_o.tile([P, 2, D], F32, name="o", tag="o")
+            o_ps[pr] = ps_o.tile([P, 2, D], F32, name="o", tag="o")
+            product_both(pr)
+
+        def product_both(pr):
             for j in range(2):
-                nc.tensor.matmul_mx(
-                    out=o[:, j, :],
-                    lhsT=a_codes[pr][:, j * P:(j + 1) * P].bitcast(FP8X4),
-                    lhsT_scale=a_scales[pr][:, j * P:(j + 1) * P],
-                    rhs=v_codes[h][:].bitcast(FP8X4),
-                    rhs_scale=v_scales[h][:],
-                    start=True, stop=True,
-                )
-            o_ps[pr] = o
+                product_half(pr, j)
+
+        def product_half(pr, j):
+            h = pr // 2
+            nc.tensor.matmul_mx(
+                out=o_ps[pr][:, j, :],
+                lhsT=a_codes[pr][:, j * P:(j + 1) * P].bitcast(FP8X4),
+                lhsT_scale=a_scales[pr][:, j * P:(j + 1) * P],
+                rhs=v_codes[h][:].bitcast(FP8X4),
+                rhs_scale=v_scales[h][:],
+                start=True, stop=True,
+            )
 
         def ln_stats(pr):
             st = sm.tile([P, 6], F32, name="st", tag="st")
@@ -272,6 +310,28 @@ def tile_differentialattention_t_kernel(tc, query, key, value, lambda_params, ou
                 out=ov[h].rearrange("(p t) d -> p t d", t=QB)[:, 2 * half:2 * half + 2, :], in_=ob[:]
             )
 
+        def ln_coeffs_drain(pr):
+            sd = sm.tile([P, 2, 1], F32, name="sd", tag="sd")
+            nc.scalar.activation(
+                out=sd[:], in_=mv[pr][:, :, 2:3], func=ACT.Sqrt, bias=eps_g[:, 0, :],
+                scale=1.0 / (D * GAIN * GAIN),
+            )
+            rs = sm.tile([P, 2, 1], F32, name="rs", tag="rs")
+            nc.vector.reciprocal(out=rs[:], in_=sd[:])
+            ln_scale[pr] = rs
+
+        def ln_apply_last(pr):
+            h, half = divmod(pr, 2)
+            ob = op.tile([P, 2, D], F32, name="ob", tag="ob")
+            for j in range(2):
+                nc.vector.tensor_scalar(
+                    out=ob[:, j, :], in0=o_ps[pr][:, j, :], scalar1=mv[pr][:, j, 1:2],
+                    scalar2=ln_scale[pr][:, j, :], op0=ALU.subtract, op1=ALU.mult,
+                )
+                nc.sync.dma_start(
+                    out=ov[h].rearrange("(p t) d -> p t d", t=QB)[:, 2 * half + j, :], in_=ob[:, j, :]
+                )
+
         def unit_ok(u):
             return 0 <= u < UNITS
 
@@ -296,12 +356,12 @@ def tile_differentialattention_t_kernel(tc, query, key, value, lambda_params, ou
         for h in range(1, 3):
             load_qk(h)
             load_v(h)
-        for w in range(5):
+        for w in range(3):
             wp = ps_t.tile([P, S], F32, name="wp", tag="tr")
             nc.tensor.matmul(wp[:], lhsT=zeros[:, 0:P], rhs=zeros[:], start=True, stop=True)
         flip_first()
         scores(0)
-        for i in range(UNITS + 10):
+        for i in range(UNITS):
             h = head_due(i, -11)
             if h >= 0:
                 load_qk(h)
@@ -309,7 +369,7 @@ def tile_differentialattention_t_kernel(tc, query, key, value, lambda_params, ou
 
             if unit_ok(i - 2):
                 recip(i - 2)
-                scale2(i - 2)
+                scale2(i - 2, nc.gpsimd)
             if unit_ok(i):
                 row_max(i)
             pr = pair_due(i, 9)
@@ -364,3 +424,40 @@ def tile_differentialattention_t_kernel(tc, query, key, value, lambda_params, ou
                 kT[hk] = flip_out(flipped, "kT")
             if pr >= 0:
                 product(pr)
+
+        nc.scalar.activation(out=sqrt_warm[:], in_=eps_g[:], func=ACT.Sqrt)
+        last = UNITS - 1
+        pl = PAIRS - 1
+        recip(last - 1)
+        recip(last)
+        scale2(last - 1, nc.vector)
+        scale2(last, nc.vector)
+        attn_round(last - 1)
+        ln_shift(pl - 3)
+        attn_round(last)
+        attn_flip(last - 2)
+        attn_out(last - 2)
+        attn_flip_rounded(last - 1)
+        attn_out(last - 1)
+        ln_apply(pl - 3)
+        attn_flip_rounded(last)
+        ln_stats(pl - 2)
+        attn_quant(pl - 1)
+        o_ps[pl - 1] = ps_s.tile([P, 2, D], F32, name="ol", tag="s")
+        product_both(pl - 1)
+        attn_quant_half(pl, 0)
+        o_ps[pl] = ps_s.tile([P, 2, D], F32, name="ol", tag="s")
+        product_half(pl, 0)
+        ln_coeffs_drain(pl - 2)
+        ln_shift(pl - 2)
+        attn_out(last)
+        attn_quant_half(pl, 1)
+        product_half(pl, 1)
+        ln_apply(pl - 2)
+        ln_stats(pl - 1)
+        ln_stats(pl)
+        ln_coeffs_drain(pl - 1)
+        ln_shift(pl - 1)
+        ln_coeffs_drain(pl)
+        ln_apply(pl - 1)
+        ln_apply_last(pl)

@@ -55,6 +55,8 @@ def tile_differentialattention_t_kernel(tc, query, key, value, lambda_params, ou
         make_identity(nc, ident_f[:])
         neghalf = const.tile([P, 2, 1], F32, name="neghalf")
         nc.gpsimd.memset(neghalf[:], -0.5)
+        negone = const.tile([P, 2, 1], F32, name="negone")
+        nc.gpsimd.memset(negone[:], -1.0)
 
         eps_g = const.tile([P, 2, 1], F32, name="eps_g")
         nc.gpsimd.tensor_scalar(
@@ -287,8 +289,13 @@ def tile_differentialattention_t_kernel(tc, query, key, value, lambda_params, ou
                 op0=ALU.mult, op1=ALU.add,
             )
             rs = sm.tile([P, 2, 1], F32, name="rs", tag="rs")
+            nm = sm.tile([P, 2, 1], F32, name="nm", tag="nm")
+            nc.gpsimd.tensor_tensor(out=nm[:], in0=m[:, :, 1:2], in1=negone[:], op=ALU.mult)
             nc.gpsimd.tensor_tensor(out=rs[:], in0=a[:], in1=neghalf[:], op=ALU.pow)
+            lb = sm.tile([P, 2, 1], F32, name="lb", tag="lb")
+            nc.gpsimd.tensor_tensor(out=lb[:], in0=nm[:], in1=rs[:], op=ALU.mult)
             ln_scale[pr] = rs
+            ln_bias[pr] = lb
 
         def ln_shift(pr):
             lb = sm.tile([P, 2, 1], F32, name="lb", tag="lb")
@@ -382,12 +389,9 @@ def tile_differentialattention_t_kernel(tc, query, key, value, lambda_params, ou
                 ln_stats(pr)
             if unit_ok(i - 3):
                 attn_flip(i - 3)
-            pr = pair_due(i, 7)
+            pr = pair_due(i, 6)
             if pr >= 0:
                 ln_coeffs(pr)
-            pr = pair_due(i, 8)
-            if pr >= 0:
-                ln_shift(pr)
             if unit_ok(i):
                 exps(i)
             hq = 1 if i == 1 else head_due(i, -6)
@@ -433,7 +437,6 @@ def tile_differentialattention_t_kernel(tc, query, key, value, lambda_params, ou
         scale2(last - 1, nc.vector)
         scale2(last, nc.vector)
         attn_round(last - 1)
-        ln_shift(pl - 3)
         attn_round(last)
         attn_flip(last - 2)
         attn_out(last - 2)

@@ -87,6 +87,7 @@ def tile_differentialattention_t_kernel(tc, query, key, value, lambda_params, ou
         o_ps = {}
         mv = {}
         ln_scale = {}
+        sqrt_of = {}
         ln_bias = {}
 
         def load_qk(h):
@@ -317,14 +318,17 @@ def tile_differentialattention_t_kernel(tc, query, key, value, lambda_params, ou
                 out=ov[h].rearrange("(p t) d -> p t d", t=QB)[:, 2 * half:2 * half + 2, :], in_=ob[:]
             )
 
-        def ln_coeffs_drain(pr):
+        def ln_sqrt_drain(pr):
             sd = sm.tile([P, 2, 1], F32, name="sd", tag="sd")
             nc.scalar.activation(
                 out=sd[:], in_=mv[pr][:, :, 2:3], func=ACT.Sqrt, bias=eps_g[:, 0, :],
                 scale=1.0 / (D * GAIN * GAIN),
             )
+            sqrt_of[pr] = sd
+
+        def ln_recip_drain(pr):
             rs = sm.tile([P, 2, 1], F32, name="rs", tag="rs")
-            nc.vector.reciprocal(out=rs[:], in_=sd[:])
+            nc.vector.reciprocal(out=rs[:], in_=sqrt_of[pr][:])
             ln_scale[pr] = rs
 
         def ln_apply_last(pr):
@@ -389,8 +393,7 @@ def tile_differentialattention_t_kernel(tc, query, key, value, lambda_params, ou
                 ln_stats(pr)
             if unit_ok(i - 3):
                 attn_flip(i - 3)
-            pr = pair_due(i, 6)
-            if pr >= 0:
+            if 0 <= pr < PAIRS - 4:
                 ln_coeffs(pr)
             if unit_ok(i):
                 exps(i)
@@ -442,7 +445,6 @@ def tile_differentialattention_t_kernel(tc, query, key, value, lambda_params, ou
         attn_out(last - 2)
         attn_flip_rounded(last - 1)
         attn_out(last - 1)
-        ln_apply(pl - 3)
         attn_flip_rounded(last)
         ln_stats(pl - 2)
         attn_quant(pl - 1)
@@ -451,16 +453,23 @@ def tile_differentialattention_t_kernel(tc, query, key, value, lambda_params, ou
         attn_quant_half(pl, 0)
         o_ps[pl] = ps_s.tile([P, 2, D], F32, name="ol", tag="s")
         product_half(pl, 0)
-        ln_coeffs_drain(pl - 2)
+        ln_sqrt_drain(pl - 3)
+        ln_sqrt_drain(pl - 2)
+        ln_recip_drain(pl - 3)
+        ln_recip_drain(pl - 2)
+        ln_shift(pl - 3)
         ln_shift(pl - 2)
         attn_out(last)
         attn_quant_half(pl, 1)
         product_half(pl, 1)
-        ln_apply(pl - 2)
+        ln_apply(pl - 3)
         ln_stats(pl - 1)
+        ln_apply(pl - 2)
         ln_stats(pl)
-        ln_coeffs_drain(pl - 1)
+        ln_sqrt_drain(pl - 1)
+        ln_sqrt_drain(pl)
+        ln_recip_drain(pl - 1)
+        ln_recip_drain(pl)
         ln_shift(pl - 1)
-        ln_coeffs_drain(pl)
-        ln_apply(pl - 1)
         ln_apply_last(pl)
+        ln_apply(pl - 1)

from contextlib import ExitStack
import math

import concourse.mybir as mybir
from concourse.masks import make_identity

F32 = mybir.dt.float32
BF16 = mybir.dt.bfloat16
U32 = mybir.dt.uint32
U8 = mybir.dt.uint8
FP8X4 = mybir.dt.float8_e4m3fn_x4
ALU = mybir.AluOpType
ACT = mybir.ActivationFunctionType
AX = mybir.AxisListType

P = 128
HEADS = 16
S = 512
D = 256
D2 = 128
QB = 4
UNITS = HEADS * QB
PAIRS = UNITS // 2
SCALE = 1.0 / math.sqrt(D2)
EPS = 1e-5
GAIN = 1.0 - 0.8
FLOPS = HEADS * (2 * 2 * S * S * D2 + 2 * S * S * D)


def tile_differentialattention_t_kernel(tc, query, key, value, lambda_params, out):
    nc = tc.nc
    qv = query.rearrange("b h s d -> (b h) s d")
    kv = key.rearrange("b h s d -> (b h) s d")
    vv = value.rearrange("b h s d -> (b h) s d")
    ov = out.rearrange("b h s d -> (b h) s d")

    with ExitStack() as ctx:
        const = ctx.enter_context(tc.tile_pool(name="const", bufs=1))
        ld = ctx.enter_context(tc.tile_pool(name="ld", bufs=4))
        tsb = ctx.enter_context(tc.tile_pool(name="tsb", bufs=3))
        vq = ctx.enter_context(tc.tile_pool(name="vq", bufs=3))
        ep = ctx.enter_context(tc.tile_pool(name="ep", bufs=6))
        gp = ctx.enter_context(tc.tile_pool(name="gp", bufs=3))
        sm = ctx.enter_context(tc.tile_pool(name="sm", bufs=8))
        op = ctx.enter_context(tc.tile_pool(name="op", bufs=4))
        ps_s = ctx.enter_context(tc.psum_pool(name="ps_s", bufs=4))
        ps_t = ctx.enter_context(tc.psum_pool(name="ps_t", bufs=2))
        ps_o = ctx.enter_context(tc.psum_pool(name="ps_o", bufs=2))

        zeros = const.tile([P, S], BF16, name="zeros")
        nc.vector.memset(zeros[:], 0.0)
        ident = const.tile([P, P], BF16, name="ident")
        make_identity(nc, ident[:])
        ident_f = const.tile([P, P], F32, name="ident_f")
        make_identity(nc, ident_f[:])
        neghalf = const.tile([P, 2, 1], F32, name="neghalf")
        nc.gpsimd.memset(neghalf[:], -0.5)
        negone = const.tile([P, 2, 1], F32, name="negone")
        nc.gpsimd.memset(negone[:], -1.0)

        eps_g = const.tile([P, 2, 1], F32, name="eps_g")
        nc.gpsimd.tensor_scalar(
            out=eps_g[:], in0=neghalf[:], scalar1=0.0, scalar2=EPS / (GAIN * GAIN), op0=ALU.mult, op1=ALU.add
        )
        sqrt_warm = const.tile([P, 2, 1], F32, name="sqrt_warm")

        ctx.enter_context(tc.manual_schedule())

        q_sb = {}
        k_sb = {}
        v_sb = {}
        qT = {}
        kT = {}
        v_grp = {}
        v_codes = {}
        v_scales = {}
        s_ps = {}
        nbias = {}
        sums = {}
        rec = {}
        e_sb = {}
        aT = {}
        d_sb = {}
        grp = {}
        a_codes = {}
        a_scales = {}
        o_ps = {}
        mv = {}
        ln_scale = {}
        sqrt_of = {}
        ln_bias = {}

        def load_qk(h):
            tk = ld.tile([P, QB, D], BF16, name="tk", tag="k")
            nc.sync.dma_start(out=tk[:], in_=kv[h].rearrange("(t p) d -> p t d", p=P))
            tq = ld.tile([P, QB, D], BF16, name="tq", tag="q")
            nc.sync.dma_start(out=tq[:], in_=qv[h].rearrange("(p t) d -> p t d", t=QB))
            q_sb[h] = tq
            k_sb[h] = tk

        def load_v(h):
            tv = ld.tile([P, QB, D], BF16, name="tv", tag="v")
            nc.sync.dma_start(out=tv[:], in_=vv[h].rearrange("(t p) d -> p t d", p=P))
            v_sb[h] = tv

        def flip_pe(src):
            tp = ps_t.tile([P, 2, S], BF16, name="tp", tag="tr")
            for hf in range(2):
                for t in range(QB):
                    nc.tensor.transpose(
                        tp[:, hf, t * P:(t + 1) * P], src[:, t, hf * D2:(hf + 1) * D2], ident[:]
                    )
            return tp

        def flip_first():
            kT[0] = tsb.tile([P, 2, S], BF16, name="dst", tag="kT")
            qT[0] = tsb.tile([P, 2, S], BF16, name="dst", tag="qT")
            for hf in range(2):
                for src, dst, copy in (
                    (k_sb[0], kT[0], nc.vector.tensor_copy), (q_sb[0], qT[0], nc.scalar.copy)
                ):
                    tp = ps_s.tile([P, S], BF16, name="tph", tag="s")
                    for t in range(QB):
                        nc.tensor.transpose(
                            tp[:, t * P:(t + 1) * P], src[:, t, hf * D2:(hf + 1) * D2], ident[:]
                        )
                    copy(out=dst[:, hf, :], in_=tp[:])
                if hf == 0:
                    value_group(0, 0)

        def flip_out(tp, tag):
            dst = tsb.tile([P, 2, S], BF16, name="dst", tag=tag)
            nc.scalar.copy(out=dst[:], in_=tp[:])
            return dst

        def value_group(h, half):
            if half == 0:
                vg = vq.tile([P, D, 4], BF16, name="vg", tag="vg", align_bytes=64)
                v_grp[h] = vg
            cols = slice(half * P, (half + 1) * P)
            nc.vector.tensor_copy(
                out=v_grp[h][:, cols, :].rearrange("p (c i) t -> p c t i", i=4),
                in_=v_sb[h][:, :, cols].rearrange("p t (c i) -> p c t i", i=4),
            )

        def value_quant(h, half):
            if half == 0:
                vc = vq.tile([P, D], U32, name="vc", tag="vc", align_bytes=64)
                vs = vq.tile([P, D], U8, name="vs", tag="vs", align_bytes=64)
                v_codes[h] = vc
                v_scales[h] = vs
            cols = slice(half * P, (half + 1) * P)
            nc.vector.quantize_mx(
                out=v_codes[h][:, cols].bitcast(FP8X4), scales=v_scales[h][:, cols],
                in_=v_grp[h][:, cols, :].rearrange("p f t -> p (f t)"),
            )

        def scores(u):
            h, t = divmod(u, QB)
            for hf in range(2):
                sp = ps_s.tile([P, S], F32, name="sp", tag="s")
                nc.tensor.matmul(
                    sp[:], lhsT=qT[h][:, hf, t * P:(t + 1) * P], rhs=kT[h][:, hf, :],
                    start=True, stop=True,
                )
                s_ps[(u, hf)] = sp

        def row_max(u):
            nb = sm.tile([P, 2], F32, name="nb", tag="nb")
            for hf in range(2):
                x = ep.tile([P, S], F32, name="x", tag="e%d" % hf)
                nc.vector.tensor_scalar(
                    out=x[:], in0=s_ps[(u, hf)][:], scalar1=-SCALE, scalar2=None,
                    op0=ALU.mult, op1=ALU.min, accum_out=nb[:, hf:hf + 1],
                )
                e_sb[(u, hf)] = x
            nbias[u] = nb

        def exps(u):
            su = sm.tile([P, 2], F32, name="su", tag="su")
            for hf in range(2):
                e = e_sb[(u, hf)]
                nc.scalar.activation(
                    out=e[:], in_=e[:], func=ACT.Exp,
                    bias=nbias[u][:, hf:hf + 1], scale=-1.0, accum_out=su[:, hf:hf + 1],
                )
            sums[u] = su

        def recip(u):
            r = sm.tile([P, 2], F32, name="r", tag="r")
            nc.vector.reciprocal(out=r[:], in_=sums[u][:])
            rec[u] = r

        def scale2(u, eng):
            h = u // QB
            e2 = e_sb[(u, 1)]
            eng.tensor_scalar(
                out=e2[:], in0=e2[:], scalar1=rec[u][:, 1:2], scalar2=nlam[:, (h % 2):(h % 2) + 1],
                op0=ALU.mult, op1=ALU.mult,
            )

        def combine(u):
            e1 = e_sb[(u, 0)]
            nc.vector.tensor_scalar(
                out=e1[:], in0=e1[:], scalar1=rec[u][:, 0:1], scalar2=None, op0=ALU.mult
            )

        def attn_flip(u):
            tp = ps_t.tile([P, QB, P], F32, name="tpa", tag="tr")
            for t in range(QB):
                for hf in range(2):
                    nc.tensor.matmul(
                        tp[:, t, :], lhsT=e_sb[(u, hf)][:, t * P:(t + 1) * P], rhs=ident_f[:],
                        is_transpose=True, start=(hf == 0), stop=(hf == 1),
                    )
            aT[u] = tp

        def attn_out(u):
            pr, j = divmod(u, 2)
            if j == 0:
                g = gp.tile([P, 2, P, 4], BF16, name="g", tag="g", align_bytes=64)
                grp[pr] = g
            nc.scalar.copy(out=grp[pr][:, j, :, :], in_=aT[u][:].rearrange("p t q -> p q t"))

        def attn_round(u):
            d = op.tile([P, S], BF16, name="d", tag="d")
            nc.vector.scalar_tensor_tensor(
                out=d[:], in0=e_sb[(u, 0)][:], scalar=rec[u][:, 0:1], in1=e_sb[(u, 1)][:],
                op0=ALU.mult, op1=ALU.add,
            )
            d_sb[u] = d

        def attn_flip_rounded(u):
            tp = ps_t.tile([P, QB, P], BF16, name="tpd", tag="tr")
            for t in range(QB):
                nc.tensor.transpose(tp[:, t, :], d_sb[u][:, t * P:(t + 1) * P], ident[:])
            aT[u] = tp

        def attn_quant_half(pr, j):
            if j == 0:
                ac = gp.tile([P, 2 * P], U32, name="ac", tag="ac", align_bytes=64)
                asc = gp.tile([P, 2 * P], U8, name="asc", tag="asc", align_bytes=64)
                a_codes[pr] = ac
                a_scales[pr] = asc
            cols = slice(j * P, (j + 1) * P)
            nc.vector.quantize_mx(
                out=a_codes[pr][:, cols].bitcast(FP8X4), scales=a_scales[pr][:, cols],
                in_=grp[pr][:, j, :, :].rearrange("p q t -> p (q t)"),
            )

        def attn_quant(pr):
            ac = gp.tile([P, 2 * P], U32, name="ac", tag="ac", align_bytes=64)
            asc = gp.tile([P, 2 * P], U8, name="asc", tag="asc", align_bytes=64)
            nc.vector.quantize_mx(
                out=ac[:].bitcast(FP8X4), scales=asc[:],
                in_=grp[pr][:].rearrange("p j q t -> p (j q t)"),
            )
            a_codes[pr] = ac
            a_scales[pr] = asc

        def product(pr):
            o_ps[pr] = ps_o.tile([P, 2, D], F32, name="o", tag="o")
            product_both(pr)

        def product_both(pr):
            for j in range(2):
                product_half(pr, j)

        def product_half(pr, j):
            h = pr // 2
            nc.tensor.matmul_mx(
                out=o_ps[pr][:, j, :],
                lhsT=a_codes[pr][:, j * P:(j + 1) * P].bitcast(FP8X4),
                lhsT_scale=a_scales[pr][:, j * P:(j + 1) * P],
                rhs=v_codes[h][:].bitcast(FP8X4),
                rhs_scale=v_scales[h][:],
                start=True, stop=True,
            )

        def ln_stats(pr):
            st = sm.tile([P, 6], F32, name="st", tag="st")
            nc.vector.bn_stats(out=st[:], in_=o_ps[pr][:].rearrange("p j d -> p d j"))
            mv[pr] = st[:].rearrange("p (j s) -> p j s", s=3)

        def ln_coeffs(pr):
            m = mv[pr]
            a = sm.tile([P, 2, 1], F32, name="a", tag="a")
            nc.gpsimd.tensor_scalar(
                out=a[:], in0=m[:, :, 2:3], scalar1=1.0 / (D * GAIN * GAIN), scalar2=EPS / (GAIN * GAIN),
                op0=ALU.mult, op1=ALU.add,
            )
            rs = sm.tile([P, 2, 1], F32, name="rs", tag="rs")
            nm = sm.tile([P, 2, 1], F32, name="nm", tag="nm")
            nc.gpsimd.tensor_tensor(out=nm[:], in0=m[:, :, 1:2], in1=negone[:], op=ALU.mult)
            nc.gpsimd.tensor_tensor(out=rs[:], in0=a[:], in1=neghalf[:], op=ALU.pow)
            lb = sm.tile([P, 2, 1], F32, name="lb", tag="lb")
            nc.gpsimd.tensor_tensor(out=lb[:], in0=nm[:], in1=rs[:], op=ALU.mult)
            ln_scale[pr] = rs
            ln_bias[pr] = lb

        def ln_shift(pr):
            lb = sm.tile([P, 2, 1], F32, name="lb", tag="lb")
            nc.vector.scalar_tensor_tensor(
                out=lb[:], in0=mv[pr][:, :, 1:2], scalar=-1.0, in1=ln_scale[pr][:],
                op0=ALU.mult, op1=ALU.mult,
            )
            ln_bias[pr] = lb

        def ln_apply(pr):
            h, half = divmod(pr, 2)
            ob = op.tile([P, 2, D], F32, name="ob", tag="ob")
            for j in range(2):
                nc.scalar.activation(
                    out=ob[:, j, :], in_=o_ps[pr][:, j, :], func=ACT.Identity,
                    bias=ln_bias[pr][:, j, :], scale=ln_scale[pr][:, j, :],
                )
            nc.sync.dma_start(
                out=ov[h].rearrange("(p t) d -> p t d", t=QB)[:, 2 * half:2 * half + 2, :], in_=ob[:]
            )

        def ln_sqrt_drain(pr):
            sd = sm.tile([P, 2, 1], F32, name="sd", tag="sd")
            nc.scalar.activation(
                out=sd[:], in_=mv[pr][:, :, 2:3], func=ACT.Sqrt, bias=eps_g[:, 0, :],
                scale=1.0 / (D * GAIN * GAIN),
            )
            sqrt_of[pr] = sd

        def ln_recip_drain(pr):
            rs = sm.tile([P, 2, 1], F32, name="rs", tag="rs")
            nc.vector.reciprocal(out=rs[:], in_=sqrt_of[pr][:])
            ln_scale[pr] = rs

        def ln_apply_last(pr):
            h, half = divmod(pr, 2)
            ob = op.tile([P, 2, D], F32, name="ob", tag="ob")
            for j in range(2):
                nc.vector.tensor_scalar(
                    out=ob[:, j, :], in0=o_ps[pr][:, j, :], scalar1=mv[pr][:, j, 1:2],
                    scalar2=ln_scale[pr][:, j, :], op0=ALU.subtract, op1=ALU.mult,
                )
                nc.sync.dma_start(
                    out=ov[h].rearrange("(p t) d -> p t d", t=QB)[:, 2 * half + j, :], in_=ob[:, j, :]
                )

        def unit_ok(u):
            return 0 <= u < UNITS

        def head_due(i, off):
            if (i - off) % QB == 0 and 0 <= (i - off) // QB < HEADS:
                return (i - off) // QB
            return -1

        def pair_due(i, lag):
            if (i - lag) % 2 == 0 and 0 <= (i - lag) // 2 < PAIRS:
                return (i - lag) // 2
            return -1

        load_qk(0)
        load_v(0)
        lam_bf = const.tile([P, 2], BF16, name="lam_bf")
        nc.sync.dma_start(out=lam_bf[:], in_=lambda_params.partition_broadcast(P))
        nlam = const.tile([P, 2], F32, name="nlam")
        nc.gpsimd.tensor_scalar(
            out=nlam[:], in0=lam_bf[:], scalar1=-1.0, scalar2=0.0, op0=ALU.mult, op1=ALU.add
        )
        for h in range(1, 3):
            load_qk(h)
            load_v(h)
        for w in range(3):
            wp = ps_t.tile([P, S], F32, name="wp", tag="tr")
            nc.tensor.matmul(wp[:], lhsT=zeros[:, 0:P], rhs=zeros[:], start=True, stop=True)
        flip_first()
        scores(0)
        for i in range(UNITS):
            h = head_due(i, -11)
            if h >= 0:
                load_qk(h)
                load_v(h)

            if unit_ok(i - 2):
                recip(i - 2)
                scale2(i - 2, nc.gpsimd)
            if unit_ok(i):
                row_max(i)
            pr = pair_due(i, 9)
            if pr >= 0:
                ln_apply(pr)
            if unit_ok(i + 1):
                scores(i + 1)
            pr = pair_due(i, 6)
            if pr >= 0:
                ln_stats(pr)
            if unit_ok(i - 3):
                attn_flip(i - 3)
            if 0 <= pr < PAIRS - 4:
                ln_coeffs(pr)
            if unit_ok(i):
                exps(i)
            hq = 1 if i == 1 else head_due(i, -6)
            hk = head_due(i, -4)
            flipped = None
            if hq >= 0:
                flipped = flip_pe(q_sb[hq])
            if hk >= 0:
                flipped = flip_pe(k_sb[hk])

            h = head_due(i, 1)
            if h >= 0:
                value_quant(h, 0)
            h = head_due(i, 3)
            if h >= 0:
                value_quant(h, 1)
            pr = pair_due(i, 5)
            if pr >= 0:
                attn_quant(pr)
            if unit_ok(i - 2):
                combine(i - 2)
            h = head_due(i, 0)
            if h >= 1:
                value_group(h, 0)
            h = head_due(i, 2)
            if h >= 0:
                value_group(h, 1)

            if unit_ok(i - 3):
                attn_out(i - 3)
            if hq >= 0:
                qT[hq] = flip_out(flipped, "qT")
            if hk >= 0:
                kT[hk] = flip_out(flipped, "kT")
            if pr >= 0:
                product(pr)

        nc.scalar.activation(out=sqrt_warm[:], in_=eps_g[:], func=ACT.Sqrt)
        last = UNITS - 1
        pl = PAIRS - 1
        recip(last - 1)
        recip(last)
        scale2(last - 1, nc.vector)
        scale2(last, nc.vector)
        attn_round(last - 1)
        attn_round(last)
        attn_flip(last - 2)
        attn_out(last - 2)
        attn_flip_rounded(last - 1)
        attn_out(last - 1)
        attn_flip_rounded(last)
        ln_stats(pl - 2)
        attn_quant(pl - 1)
        o_ps[pl - 1] = ps_s.tile([P, 2, D], F32, name="ol", tag="s")
        product_both(pl - 1)
        attn_quant_half(pl, 0)
        o_ps[pl] = ps_s.tile([P, 2, D], F32, name="ol", tag="s")
        product_half(pl, 0)
        ln_sqrt_drain(pl - 3)
        ln_sqrt_drain(pl - 2)
        ln_recip_drain(pl - 3)
        ln_recip_drain(pl - 2)
        ln_shift(pl - 3)
        ln_shift(pl - 2)
        attn_out(last)
        attn_quant_half(pl, 1)
        product_half(pl, 1)
        ln_apply(pl - 3)
        ln_stats(pl - 1)
        ln_apply(pl - 2)
        ln_stats(pl)
        ln_sqrt_drain(pl - 1)
        ln_sqrt_drain(pl)
        ln_recip_drain(pl - 1)
        ln_recip_drain(pl)
        ln_shift(pl - 1)
        ln_apply_last(pl)
        ln_apply(pl - 1)
